import numpy as np
import ml_dtypes


def mxq(x, axis, fmt="e4m3"):
    dtype, down = {"e4m3": (ml_dtypes.float8_e4m3fn, 7), "e5m2": (ml_dtypes.float8_e5m2, 14)}[fmt]
    v = np.moveaxis(np.asarray(x, np.float32).astype(ml_dtypes.bfloat16).astype(np.float64), axis, -1)
    blocks = v.reshape(v.shape[:-1] + (-1, 32))
    amax = np.abs(blocks).max(-1, keepdims=True)
    byte = np.maximum(np.where(amax > 0, np.frexp(amax)[1] - 1 + 127, 0) - down, 1)
    scale = np.exp2(byte - 127.0)
    codes = (blocks / scale).astype(np.float32).astype(dtype).astype(np.float64)
    return np.moveaxis((codes * scale).reshape(v.shape), -1, axis)


WIDE = False


def mx_kscale(k):
    if not WIDE:
        return np.ones(k)
    levels = np.array([10, -10, 5, -5, 0])
    a = np.random.permutation(np.resize(levels, k // 512 * 4)).reshape(k // 512, 4)
    idx = np.arange(k)
    return np.exp2(a[idx // 512, idx % 128 // 32])


BF16 = ml_dtypes.bfloat16


def bf(x):
    return np.asarray(x, np.float32).astype(BF16)


def f64(x):
    return np.asarray(x).astype(np.float64)


B, T, G, I, H = 4, 256, 8, 512, 512


def setup_inputs():
    s = mx_kscale(I)
    return {"x": bf((np.random.standard_normal((B, T, G, I)) * s).reshape(B, T, G * I)),
            "W": bf(np.random.standard_normal((G, H, I)) / np.sqrt(I) / s),
            "b": bf(np.random.standard_normal((G, H)) * 0.5)}


def reference(x, W, b):
    xg = f64(x).reshape(B, T, G, I)
    xq = mxq(xg, 3, "e4m3")
    wq = mxq(f64(W), 2, "e4m3")
    y = xq.transpose(2, 0, 1, 3).reshape(G, B * T, I) @ wq.transpose(0, 2, 1)
    out = y.reshape(G, B, T, H).transpose(1, 2, 0, 3) + f64(b)
    return np.swapaxes(out, -1, -2).reshape(B, T, G * H)

@@ -1,0 +1,201 @@
+from contextlib import ExitStack
+
+import concourse.mybir as mybir
+from concourse.masks import make_identity
+
+F32 = mybir.dt.float32
+BF16 = mybir.dt.bfloat16
+U32 = mybir.dt.uint32
+U8 = mybir.dt.uint8
+FP8X4 = mybir.dt.float8_e4m3fn_x4
+ADD = mybir.AluOpType.add
+
+P = 128
+G = 8
+I = 512
+H = 512
+TOK = 1024
+NT = TOK // P
+FLOPS = 2 * TOK * G * I * H
+
+MANUAL = True
+VIA_S = ((0,), (0, 2), (0,), (0, 2), (0,), (0, 2), (0,), (0,))
+ORDER = {
+    (): ((0, 0), (0, 1), (1, 0), (1, 1), (2, 0), (2, 1), (3, 0), (3, 1)),
+    (0,): ((0, 0), (1, 0), (0, 1), (1, 1), (2, 0), (2, 1), (3, 0), (3, 1)),
+    (0, 2): ((0, 0), (1, 0), (0, 1), (1, 1), (2, 0), (3, 0), (2, 1), (3, 1)),
+}
+Q_AFTER = 4
+
+
+def tile_groupedlinear_kernel(tc, x, W, b, out):
+    nc = tc.nc
+    xf = x.flatten_outer_dims()
+    of = out.flatten_outer_dims()
+    with ExitStack() as ctx:
+        const = ctx.enter_context(tc.tile_pool(name="const", bufs=1))
+        raw_pool = ctx.enter_context(tc.tile_pool(name="raw", bufs=10))
+        grp_pool = ctx.enter_context(tc.tile_pool(name="grp", bufs=3))
+        xq_pool = ctx.enter_context(tc.tile_pool(name="xq", bufs=2))
+        out_pool = ctx.enter_context(tc.tile_pool(name="outp", bufs=4))
+        psum_t = ctx.enter_context(tc.psum_pool(name="pt", bufs=4))
+        psum_a = ctx.enter_context(tc.psum_pool(name="pa", bufs=4))
+        if MANUAL:
+            ctx.enter_context(tc.manual_schedule())
+
+        brow = grp_pool.tile([1, G * H], BF16, tag="grp", name="brow", align_bytes=64)
+        nc.scalar.dma_start(out=brow[:], in_=b.rearrange("(o g) h -> o (g h)", o=1))
+
+        xraw = {}
+        wraw = {}
+
+        def load_x(i):
+            t = raw_pool.tile([P, G * I], BF16, tag="raw", name="xraw%d" % i)
+            nc.sync.dma_start(out=t[:], in_=xf[i * P:(i + 1) * P, :])
+            xraw[i] = t
+
+        def load_w(j):
+            t = raw_pool.tile([P, 2 * 4 * I], BF16, tag="raw", name="wraw%d" % j)
+            nc.sync.dma_start(
+                out=t[:].rearrange("p (g c) -> p g c", g=2),
+                in_=W[2 * j:2 * j + 2].rearrange("g (p t) i -> p g (t i)", t=4))
+            wraw[j] = t
+
+        load_x(0)
+        for j in range(4):
+            load_w(j)
+        for i in range(1, NT):
+            load_x(i)
+
+        ident = const.tile([P, P], F32, name="ident")
+        make_identity(nc, ident[:])
+        ones = const.tile([P, P], BF16, name="ones")
+        nc.vector.memset(ones[:], 1.0)
+        bz = grp_pool.tile([P, G * H], BF16, tag="grp", name="bz", align_bytes=64)
+        nc.vector.memset(bz[:], 0.0)
+        nc.vector.tensor_copy(out=bz[0:1, :], in_=brow[:])
+        bzv = bz[:].rearrange("p (g h) -> p g h", g=G)
+        bias = const.tile([P, H, G], F32, name="bias")
+
+        def bias_block(hb):
+            for gh in range(2):
+                acc = psum_a.tile([P, 4, P], F32, tag="acc", name="bacc")
+                nc.tensor.matmul(
+                    out=acc[:], lhsT=ones[:],
+                    rhs=bzv[:, gh * 4:(gh + 1) * 4, hb * P:(hb + 1) * P],
+                    start=True, stop=True)
+                nc.scalar.copy(
+                    out=bias[:, hb * P:(hb + 1) * P, gh * 4:(gh + 1) * 4],
+                    in_=acc[:].rearrange("p g h -> p h g"))
+
+        xq = {}
+        xs = {}
+        xg = {}
+
+        def x_transposes(i):
+            xw = xraw[i][:].bitcast(F32)
+            g_t = grp_pool.tile([P, G * I], BF16, tag="grp", name="xg%d" % i, align_bytes=64)
+            gw = g_t[:].bitcast(F32).rearrange("p (g r u) -> p g r u", g=G, u=2)
+            for j in range(4):
+                tp = psum_t.tile([P, 2, 2, P], F32, tag="tp", name="xtp")
+                for gg in range(2):
+                    for u in range(2):
+                        c0 = (2 * j + gg) * 256 + u * P
+                        nc.tensor.transpose(tp[:, gg, u, :], xw[:, c0:c0 + P], ident[:])
+                nc.scalar.copy(out=gw[:, 2 * j:2 * j + 2], in_=tp[:].rearrange("p g u r -> p g r u"))
+            xg[i] = g_t
+
+        def x_quantise(i):
+            q = xq_pool.tile([P, G * P], U32, tag="xq", name="xq%d" % i, align_bytes=64)
+            s = xq_pool.tile([P, G * P], U8, tag="xs", name="xs%d" % i, align_bytes=64)
+            nc.vector.quantize_mx(out=q[:].bitcast(FP8X4), scales=s[:], in_=xg[i][:])
+            xq[i] = q
+            xs[i] = s
+
+        wq = {}
+        ws = {}
+        wg = {}
+
+        def w_transposes(j):
+            ww = wraw[j][:].bitcast(F32)
+            g_t = grp_pool.tile([P, 2 * H * 4], BF16, tag="grp", name="wg%d" % j, align_bytes=64)
+            gw = g_t[:].bitcast(F32).rearrange("p (g r t u) -> p g r t u", g=2, t=4, u=2)
+            for gg in range(2):
+                for tpair in range(2):
+                    tp = psum_t.tile([P, 2, 2, P], F32, tag="tp", name="wtp")
+                    for tt in range(2):
+                        for u in range(2):
+                            c0 = gg * 1024 + (2 * tpair + tt) * 256 + u * P
+                            nc.tensor.transpose(tp[:, tt, u, :], ww[:, c0:c0 + P], ident[:])
+                    dst = gw[:, gg, :, 2 * tpair:2 * tpair + 2, :]
+                    src = tp[:].rearrange("p t u r -> p r t u")
+                    if gg == 0:
+                        nc.vector.tensor_copy(out=dst, in_=src)
+                    else:
+                        nc.scalar.copy(out=dst, in_=src)
+            wg[j] = g_t
+
+        def w_quantise(j):
+            q = const.tile([P, 2 * H], U32, name="wq%d" % j, align_bytes=64)
+            s = const.tile([P, 2 * H], U8, name="ws%d" % j, align_bytes=64)
+            nc.vector.quantize_mx(out=q[:].bitcast(FP8X4), scales=s[:], in_=wg[j][:])
+            wq[j] = q
+            ws[j] = s
+
+        osb = {}
+
+        def bank(i, hb, gh):
+            acc = psum_a.tile([P, 4, P], F32, tag="acc", name="acc")
+            for g4 in range(4):
+                g = gh * 4 + g4
+                wc = (g % 2) * H + hb * P
+                nc.tensor.matmul_mx(
+                    out=acc[:, g4, :],
+                    lhsT=xq[i][:, g * P:(g + 1) * P].bitcast(FP8X4),
+                    lhsT_scale=xs[i][:, g * P:(g + 1) * P],
+                    rhs=wq[g // 2][:, wc:wc + P].bitcast(FP8X4),
+                    rhs_scale=ws[g // 2][:, wc:wc + P],
+                    start=True, stop=True)
+            hs = slice(hb * P, (hb + 1) * P)
+            gs = slice(gh * 4, (gh + 1) * 4)
+            if hb in VIA_S[i]:
+                nc.scalar.copy(out=osb[i][:, hs, gs], in_=acc[:].rearrange("p g h -> p h g"))
+                if gh == 1:
+                    o2 = osb[i][:, hs, :].rearrange("p h g -> p (h g)")
+                    nc.gpsimd.tensor_tensor(
+                        out=o2, in0=o2, in1=bias[:, hs, :].rearrange("p h g -> p (h g)"), op=ADD)
+            else:
+                nc.vector.tensor_tensor(
+                    out=osb[i][:, hs, gs], in0=acc[:].rearrange("p g h -> p h g"),
+                    in1=bias[:, hs, gs], op=ADD)
+
+        def store(i, h0, h1):
+            nc.sync.dma_start(
+                out=of[i * P:(i + 1) * P, h0 * G:h1 * G],
+                in_=osb[i][:, h0:h1, :].rearrange("p h g -> p (h g)"))
+
+        x_transposes(0)
+        for j in range(4):
+            w_transposes(j)
+            bias_block(j)
+            if j == 0:
+                x_quantise(0)
+            else:
+                w_quantise(j - 1)
+        w_quantise(3)
+
+        for i in range(NT):
+            if i + 1 < NT:
+                x_transposes(i + 1)
+            osb[i] = out_pool.tile([P, H, G], F32, tag="osb", name="osb%d" % i)
+            for n, (hb, gh) in enumerate(ORDER[VIA_S[i]]):
+                if n == Q_AFTER and i + 1 < NT:
+                    x_quantise(i + 1)
+                if n == 4:
+                    store(i, 0, 256)
+                bank(i, hb, gh)
+            if i + 1 < NT:
+                store(i, 256, 512)
+            else:
+                store(i, 256, 384)
+                store(i, 384, 512)

@@ -19,7 +19,7 @@ NT = TOK // P
 FLOPS = 2 * TOK * G * I * H
 
 MANUAL = True
-VIA_S = ((0,), (0, 2), (0,), (0, 2), (0,), (0, 2), (0,), (0,))
+VIA_S = ((), (), (), (), (), (), (), ())
 ORDER = {
     (): ((0, 0), (0, 1), (1, 0), (1, 1), (2, 0), (2, 1), (3, 0), (3, 1)),
     (0,): ((0, 0), (1, 0), (0, 1), (1, 1), (2, 0), (2, 1), (3, 0), (3, 1)),

@@ -19,13 +19,8 @@ NT = TOK // P
 FLOPS = 2 * TOK * G * I * H
 
 MANUAL = True
-VIA_S = ((), (), (), (), (), (), (), ())
-ORDER = {
-    (): ((0, 0), (0, 1), (1, 0), (1, 1), (2, 0), (2, 1), (3, 0), (3, 1)),
-    (0,): ((0, 0), (1, 0), (0, 1), (1, 1), (2, 0), (2, 1), (3, 0), (3, 1)),
-    (0, 2): ((0, 0), (1, 0), (0, 1), (1, 1), (2, 0), (3, 0), (2, 1), (3, 1)),
-}
-Q_AFTER = 4
+S_BLOCK = 2
+G_SPLIT = 2
 
 
 def tile_groupedlinear_kernel(tc, x, W, b, out):
@@ -158,12 +153,15 @@ def tile_groupedlinear_kernel(tc, x, W, b, out):
                     start=True, stop=True)
             hs = slice(hb * P, (hb + 1) * P)
             gs = slice(gh * 4, (gh + 1) * 4)
-            if hb in VIA_S[i]:
+            if hb == S_BLOCK:
                 nc.scalar.copy(out=osb[i][:, hs, gs], in_=acc[:].rearrange("p g h -> p h g"))
                 if gh == 1:
-                    o2 = osb[i][:, hs, :].rearrange("p h g -> p (h g)")
-                    nc.gpsimd.tensor_tensor(
-                        out=o2, in0=o2, in1=bias[:, hs, :].rearrange("p h g -> p (h g)"), op=ADD)
+                    step = P // G_SPLIT
+                    for k in range(G_SPLIT):
+                        ks = slice(hb * P + k * step, hb * P + (k + 1) * step)
+                        o2 = osb[i][:, ks, :].rearrange("p h g -> p (h g)")
+                        nc.gpsimd.tensor_tensor(
+                            out=o2, in0=o2, in1=bias[:, ks, :].rearrange("p h g -> p (h g)"), op=ADD)
             else:
                 nc.vector.tensor_tensor(
                     out=osb[i][:, hs, gs], in0=acc[:].rearrange("p g h -> p h g"),
@@ -182,20 +180,35 @@ def tile_groupedlinear_kernel(tc, x, W, b, out):
                 x_quantise(0)
             else:
                 w_quantise(j - 1)
+        x_transposes(1)
         w_quantise(3)
 
-        for i in range(NT):
-            if i + 1 < NT:
-                x_transposes(i + 1)
+        for i in range(NT - 1):
             osb[i] = out_pool.tile([P, H, G], F32, tag="osb", name="osb%d" % i)
-            for n, (hb, gh) in enumerate(ORDER[VIA_S[i]]):
-                if n == Q_AFTER and i + 1 < NT:
-                    x_quantise(i + 1)
-                if n == 4:
-                    store(i, 0, 256)
-                bank(i, hb, gh)
-            if i + 1 < NT:
-                store(i, 256, 512)
-            else:
-                store(i, 256, 384)
-                store(i, 384, 512)
+            bank(i, 0, 0)
+            bank(i, 0, 1)
+            bank(i, 1, 0)
+            bank(i, 1, 1)
+            store(i, 0, 256)
+            if i + 2 < NT:
+                x_transposes(i + 2)
+            x_quantise(i + 1)
+            bank(i, 2, 0)
+            bank(i, 3, 0)
+            bank(i, 2, 1)
+            bank(i, 3, 1)
+            store(i, 256, 512)
+
+        i = NT - 1
+        osb[i] = out_pool.tile([P, H, G], F32, tag="osb", name="osb%d" % i)
+        bank(i, 2, 0)
+        bank(i, 0, 0)
+        bank(i, 2, 1)
+        bank(i, 0, 1)
+        bank(i, 1, 0)
+        bank(i, 1, 1)
+        store(i, 0, 256)
+        store(i, 256, 384)
+        bank(i, 3, 0)
+        bank(i, 3, 1)
+        store(i, 384, 512)

@@ -190,13 +190,13 @@ def tile_groupedlinear_kernel(tc, x, W, b, out):
             bank(i, 1, 0)
             bank(i, 1, 1)
             store(i, 0, 256)
-            if i + 2 < NT:
-                x_transposes(i + 2)
             x_quantise(i + 1)
             bank(i, 2, 0)
             bank(i, 3, 0)
             bank(i, 2, 1)
             bank(i, 3, 1)
+            if i + 2 < NT:
+                x_transposes(i + 2)
             store(i, 256, 512)
 
         i = NT - 1

@@ -20,6 +20,7 @@ FLOPS = 2 * TOK * G * I * H
 
 MANUAL = True
 S_BLOCK = 2
+BIG_STORES = 3
 G_SPLIT = 2
 
 
@@ -52,8 +53,7 @@ def tile_groupedlinear_kernel(tc, x, W, b, out):
         def load_w(j):
             t = raw_pool.tile([P, 2 * 4 * I], BF16, tag="raw", name="wraw%d" % j)
             nc.sync.dma_start(
-                out=t[:].rearrange("p (g c) -> p g c", g=2),
-                in_=W[2 * j:2 * j + 2].rearrange("g (p t) i -> p g (t i)", t=4))
+                out=t[:], in_=W[2 * j:2 * j + 2].rearrange("g (q t) i -> (g q) (t i)", t=8))
             wraw[j] = t
 
         load_x(0)
@@ -114,20 +114,19 @@ def tile_groupedlinear_kernel(tc, x, W, b, out):
         def w_transposes(j):
             ww = wraw[j][:].bitcast(F32)
             g_t = grp_pool.tile([P, 2 * H * 4], BF16, tag="grp", name="wg%d" % j, align_bytes=64)
-            gw = g_t[:].bitcast(F32).rearrange("p (g r t u) -> p g r t u", g=2, t=4, u=2)
-            for gg in range(2):
-                for tpair in range(2):
-                    tp = psum_t.tile([P, 2, 2, P], F32, tag="tp", name="wtp")
-                    for tt in range(2):
-                        for u in range(2):
-                            c0 = gg * 1024 + (2 * tpair + tt) * 256 + u * P
-                            nc.tensor.transpose(tp[:, tt, u, :], ww[:, c0:c0 + P], ident[:])
-                    dst = gw[:, gg, :, 2 * tpair:2 * tpair + 2, :]
-                    src = tp[:].rearrange("p t u r -> p r t u")
-                    if gg == 0:
-                        nc.vector.tensor_copy(out=dst, in_=src)
-                    else:
-                        nc.scalar.copy(out=dst, in_=src)
+            gw = g_t[:].bitcast(F32).rearrange("p (r t u) -> p r t u", t=8, u=2)
+            for tpair in range(4):
+                tp = psum_t.tile([P, 2, 2, P], F32, tag="tp", name="wtp")
+                for tt in range(2):
+                    for u in range(2):
+                        c0 = (2 * tpair + tt) * 256 + u * P
+                        nc.tensor.transpose(tp[:, tt, u, :], ww[:, c0:c0 + P], ident[:])
+                dst = gw[:, :, 2 * tpair:2 * tpair + 2, :]
+                src = tp[:].rearrange("p t u r -> p r t u")
+                if tpair < 2:
+                    nc.vector.tensor_copy(out=dst, in_=src)
+                else:
+                    nc.scalar.copy(out=dst, in_=src)
             wg[j] = g_t
 
         def w_quantise(j):
@@ -189,7 +188,8 @@ def tile_groupedlinear_kernel(tc, x, W, b, out):
             bank(i, 0, 1)
             bank(i, 1, 0)
             bank(i, 1, 1)
-            store(i, 0, 256)
+            if i >= BIG_STORES:
+                store(i, 0, 256)
             x_quantise(i + 1)
             bank(i, 2, 0)
             bank(i, 3, 0)
@@ -197,7 +197,10 @@ def tile_groupedlinear_kernel(tc, x, W, b, out):
             bank(i, 3, 1)
             if i + 2 < NT:
                 x_transposes(i + 2)
-            store(i, 256, 512)
+            if i >= BIG_STORES:
+                store(i, 256, 512)
+            else:
+                store(i, 0, 512)
 
         i = NT - 1
         osb[i] = out_pool.tile([P, H, G], F32, tag="osb", name="osb%d" % i)

@@ -19,7 +19,7 @@ NT = TOK // P
 FLOPS = 2 * TOK * G * I * H
 
 MANUAL = True
-S_BLOCK = 2
+S_BLOCK = 1
 BIG_STORES = 3
 G_SPLIT = 2
 
@@ -67,21 +67,20 @@ def tile_groupedlinear_kernel(tc, x, W, b, out):
         ones = const.tile([P, P], BF16, name="ones")
         nc.vector.memset(ones[:], 1.0)
         bz = grp_pool.tile([P, G * H], BF16, tag="grp", name="bz", align_bytes=64)
-        nc.vector.memset(bz[:], 0.0)
+        nc.vector.memset(bz[:].bitcast(U32), 0)
         nc.vector.tensor_copy(out=bz[0:1, :], in_=brow[:])
         bzv = bz[:].rearrange("p (g h) -> p g h", g=G)
-        bias = const.tile([P, H, G], F32, name="bias")
+        bias = const.tile([P, H, G], BF16, name="bias")
 
         def bias_block(hb):
+            acc = psum_a.tile([P, G, P], BF16, tag="acc", name="bacc")
             for gh in range(2):
-                acc = psum_a.tile([P, 4, P], F32, tag="acc", name="bacc")
                 nc.tensor.matmul(
-                    out=acc[:], lhsT=ones[:],
+                    out=acc[:, gh * 4:(gh + 1) * 4, :], lhsT=ones[:],
                     rhs=bzv[:, gh * 4:(gh + 1) * 4, hb * P:(hb + 1) * P],
                     start=True, stop=True)
-                nc.scalar.copy(
-                    out=bias[:, hb * P:(hb + 1) * P, gh * 4:(gh + 1) * 4],
-                    in_=acc[:].rearrange("p g h -> p h g"))
+            nc.scalar.copy(
+                out=bias[:, hb * P:(hb + 1) * P, :], in_=acc[:].rearrange("p g h -> p h g"))
 
         xq = {}
         xs = {}
@@ -188,12 +187,12 @@ def tile_groupedlinear_kernel(tc, x, W, b, out):
             bank(i, 0, 1)
             bank(i, 1, 0)
             bank(i, 1, 1)
-            if i >= BIG_STORES:
-                store(i, 0, 256)
             x_quantise(i + 1)
             bank(i, 2, 0)
-            bank(i, 3, 0)
             bank(i, 2, 1)
+            if i >= BIG_STORES:
+                store(i, 0, 256)
+            bank(i, 3, 0)
             bank(i, 3, 1)
             if i + 2 < NT:
                 x_transposes(i + 2)
@@ -204,12 +203,12 @@ def tile_groupedlinear_kernel(tc, x, W, b, out):
 
         i = NT - 1
         osb[i] = out_pool.tile([P, H, G], F32, tag="osb", name="osb%d" % i)
-        bank(i, 2, 0)
-        bank(i, 0, 0)
-        bank(i, 2, 1)
-        bank(i, 0, 1)
         bank(i, 1, 0)
+        bank(i, 0, 0)
         bank(i, 1, 1)
+        bank(i, 0, 1)
+        bank(i, 2, 0)
+        bank(i, 2, 1)
         store(i, 0, 256)
         store(i, 256, 384)
         bank(i, 3, 0)

@@ -20,17 +20,17 @@ FLOPS = 2 * TOK * G * I * H
 
 MANUAL = True
 S_BLOCK = 1
-BIG_STORES = 3
+BIG_STORES = 5
 G_SPLIT = 2
 
 
 def tile_groupedlinear_kernel(tc, x, W, b, out):
     nc = tc.nc
-    xf = x.flatten_outer_dims()
-    of = out.flatten_outer_dims()
+    xf = x.flatten_outer_dims().rearrange("(n p t) k -> n p t k", p=P, t=2)
+    of = out.flatten_outer_dims().rearrange("(n p t) c -> n p t c", p=P, t=2)
     with ExitStack() as ctx:
         const = ctx.enter_context(tc.tile_pool(name="const", bufs=1))
-        raw_pool = ctx.enter_context(tc.tile_pool(name="raw", bufs=10))
+        raw_pool = ctx.enter_context(tc.tile_pool(name="raw", bufs=4))
         grp_pool = ctx.enter_context(tc.tile_pool(name="grp", bufs=3))
         xq_pool = ctx.enter_context(tc.tile_pool(name="xq", bufs=2))
         out_pool = ctx.enter_context(tc.tile_pool(name="outp", bufs=4))
@@ -45,10 +45,14 @@ def tile_groupedlinear_kernel(tc, x, W, b, out):
         xraw = {}
         wraw = {}
 
-        def load_x(i):
-            t = raw_pool.tile([P, G * I], BF16, tag="raw", name="xraw%d" % i)
-            nc.sync.dma_start(out=t[:], in_=xf[i * P:(i + 1) * P, :])
-            xraw[i] = t
+        def x_pair(n):
+            t = raw_pool.tile([P, 2, G * I], BF16, tag="xraw", name="xraw%d" % n)
+            xraw[2 * n] = t[:, 0, :]
+            xraw[2 * n + 1] = t[:, 1, :]
+            return t
+
+        def load_x_pair(n):
+            nc.sync.dma_start(out=x_pair(n)[:], in_=xf[n])
 
         def load_w(j):
             t = raw_pool.tile([P, 2 * 4 * I], BF16, tag="raw", name="wraw%d" % j)
@@ -56,11 +60,13 @@ def tile_groupedlinear_kernel(tc, x, W, b, out):
                 out=t[:], in_=W[2 * j:2 * j + 2].rearrange("g (q t) i -> (g q) (t i)", t=8))
             wraw[j] = t
 
-        load_x(0)
+        first = x_pair(0)
+        nc.sync.dma_start(out=first[:, 0, :], in_=xf[0, :, 0, :])
         for j in range(4):
             load_w(j)
-        for i in range(1, NT):
-            load_x(i)
+        nc.sync.dma_start(out=first[:, 1, :], in_=xf[0, :, 1, :])
+        for n in range(1, NT // 2):
+            load_x_pair(n)
 
         ident = const.tile([P, P], F32, name="ident")
         make_identity(nc, ident[:])
@@ -87,7 +93,7 @@ def tile_groupedlinear_kernel(tc, x, W, b, out):
         xg = {}
 
         def x_transposes(i):
-            xw = xraw[i][:].bitcast(F32)
+            xw = xraw[i].bitcast(F32)
             g_t = grp_pool.tile([P, G * I], BF16, tag="grp", name="xg%d" % i, align_bytes=64)
             gw = g_t[:].bitcast(F32).rearrange("p (g r u) -> p g r u", g=G, u=2)
             for j in range(4):
@@ -167,7 +173,7 @@ def tile_groupedlinear_kernel(tc, x, W, b, out):
 
         def store(i, h0, h1):
             nc.sync.dma_start(
-                out=of[i * P:(i + 1) * P, h0 * G:h1 * G],
+                out=of[i // 2, :, i % 2, h0 * G:h1 * G],
                 in_=osb[i][:, h0:h1, :].rearrange("p h g -> p (h g)"))
 
         x_transposes(0)

@@ -92,18 +92,18 @@ def tile_groupedlinear_kernel(tc, x, W, b, out):
         xs = {}
         xg = {}
 
-        def x_transposes(i):
+        def x_transposes(i, half):
             xw = xraw[i].bitcast(F32)
-            g_t = grp_pool.tile([P, G * I], BF16, tag="grp", name="xg%d" % i, align_bytes=64)
-            gw = g_t[:].bitcast(F32).rearrange("p (g r u) -> p g r u", g=G, u=2)
-            for j in range(4):
+            if half == 0:
+                xg[i] = grp_pool.tile([P, G * I], BF16, tag="grp", name="xg%d" % i, align_bytes=64)
+            gw = xg[i][:].bitcast(F32).rearrange("p (g r u) -> p g r u", g=G, u=2)
+            for j in range(2 * half, 2 * half + 2):
                 tp = psum_t.tile([P, 2, 2, P], F32, tag="tp", name="xtp")
                 for gg in range(2):
                     for u in range(2):
                         c0 = (2 * j + gg) * 256 + u * P
                         nc.tensor.transpose(tp[:, gg, u, :], xw[:, c0:c0 + P], ident[:])
                 nc.scalar.copy(out=gw[:, 2 * j:2 * j + 2], in_=tp[:].rearrange("p g u r -> p g r u"))
-            xg[i] = g_t
 
         def x_quantise(i):
             q = xq_pool.tile([P, G * P], U32, tag="xq", name="xq%d" % i, align_bytes=64)
@@ -176,7 +176,8 @@ def tile_groupedlinear_kernel(tc, x, W, b, out):
                 out=of[i // 2, :, i % 2, h0 * G:h1 * G],
                 in_=osb[i][:, h0:h1, :].rearrange("p h g -> p (h g)"))
 
-        x_transposes(0)
+        x_transposes(0, 0)
+        x_transposes(0, 1)
         for j in range(4):
             w_transposes(j)
             bias_block(j)
@@ -184,7 +185,8 @@ def tile_groupedlinear_kernel(tc, x, W, b, out):
                 x_quantise(0)
             else:
                 w_quantise(j - 1)
-        x_transposes(1)
+        x_transposes(1, 0)
+        x_transposes(1, 1)
         w_quantise(3)
 
         for i in range(NT - 1):
@@ -194,6 +196,8 @@ def tile_groupedlinear_kernel(tc, x, W, b, out):
             bank(i, 1, 0)
             bank(i, 1, 1)
             x_quantise(i + 1)
+            if i + 2 < NT:
+                x_transposes(i + 2, 0)
             bank(i, 2, 0)
             bank(i, 2, 1)
             if i >= BIG_STORES:
@@ -201,7 +205,7 @@ def tile_groupedlinear_kernel(tc, x, W, b, out):
             bank(i, 3, 0)
             bank(i, 3, 1)
             if i + 2 < NT:
-                x_transposes(i + 2)
+                x_transposes(i + 2, 1)
             if i >= BIG_STORES:
                 store(i, 256, 512)
             else:

@@ -46,7 +46,7 @@ def tile_groupedlinear_kernel(tc, x, W, b, out):
         wraw = {}
 
         def x_pair(n):
-            t = raw_pool.tile([P, 2, G * I], BF16, tag="xraw", name="xraw%d" % n)
+            t = raw_pool.tile([P, 2, G * I], BF16, tag="xraw", name="xraw%d" % n, align_bytes=256)
             xraw[2 * n] = t[:, 0, :]
             xraw[2 * n + 1] = t[:, 1, :]
             return t
@@ -55,7 +55,7 @@ def tile_groupedlinear_kernel(tc, x, W, b, out):
             nc.sync.dma_start(out=x_pair(n)[:], in_=xf[n])
 
         def load_w(j):
-            t = raw_pool.tile([P, 2 * 4 * I], BF16, tag="raw", name="wraw%d" % j)
+            t = raw_pool.tile([P, 2 * 4 * I], BF16, tag="raw", name="wraw%d" % j, align_bytes=256)
             nc.sync.dma_start(
                 out=t[:], in_=W[2 * j:2 * j + 2].rearrange("g (q t) i -> (g q) (t i)", t=8))
             wraw[j] = t
@@ -190,7 +190,7 @@ def tile_groupedlinear_kernel(tc, x, W, b, out):
         w_quantise(3)
 
         for i in range(NT - 1):
-            osb[i] = out_pool.tile([P, H, G], F32, tag="osb", name="osb%d" % i)
+            osb[i] = out_pool.tile([P, H, G], F32, tag="osb", name="osb%d" % i, align_bytes=256)
             bank(i, 0, 0)
             bank(i, 0, 1)
             bank(i, 1, 0)
@@ -212,7 +212,7 @@ def tile_groupedlinear_kernel(tc, x, W, b, out):
                 store(i, 0, 512)
 
         i = NT - 1
-        osb[i] = out_pool.tile([P, H, G], F32, tag="osb", name="osb%d" % i)
+        osb[i] = out_pool.tile([P, H, G], F32, tag="osb", name="osb%d" % i, align_bytes=256)
         bank(i, 1, 0)
         bank(i, 0, 0)
         bank(i, 1, 1)

@@ -20,14 +20,19 @@ FLOPS = 2 * TOK * G * I * H
 
 MANUAL = True
 S_BLOCK = 1
-BIG_STORES = 5
+BIG_STORES = 6
 G_SPLIT = 2
 
 
 def tile_groupedlinear_kernel(tc, x, W, b, out):
     nc = tc.nc
-    xf = x.flatten_outer_dims().rearrange("(n p t) k -> n p t k", p=P, t=2)
-    of = out.flatten_outer_dims().rearrange("(n p t) c -> n p t c", p=P, t=2)
+    xf = x.flatten_outer_dims()
+    of = out.flatten_outer_dims()
+    half = TOK // 2
+    x_low = xf[0:half, :].rearrange("(n p t) k -> n p t k", p=P, t=2)
+    o_low = of[0:half, :].rearrange("(n p t) c -> n p t c", p=P, t=2)
+    x_high = xf[half:TOK, :].rearrange("(p t) k -> p t k", t=4)
+    o_high = of[half:TOK, :].rearrange("(p t) c -> p t c", t=4)
     with ExitStack() as ctx:
         const = ctx.enter_context(tc.tile_pool(name="const", bufs=1))
         raw_pool = ctx.enter_context(tc.tile_pool(name="raw", bufs=4))
@@ -46,13 +51,16 @@ def tile_groupedlinear_kernel(tc, x, W, b, out):
         wraw = {}
 
         def x_pair(n):
-            t = raw_pool.tile([P, 2, G * I], BF16, tag="xraw", name="xraw%d" % n, align_bytes=256)
+            t = raw_pool.tile([P, 2, G * I], BF16, tag="xraw", bufs=2, name="xraw%d" % n, align_bytes=256)
             xraw[2 * n] = t[:, 0, :]
             xraw[2 * n + 1] = t[:, 1, :]
             return t
 
-        def load_x_pair(n):
-            nc.sync.dma_start(out=x_pair(n)[:], in_=xf[n])
+        def load_x_quad():
+            t = raw_pool.tile([P, 4, G * I], BF16, tag="xquad", bufs=1, name="xquad", align_bytes=256)
+            for k in range(4):
+                xraw[4 + k] = t[:, k, :]
+            nc.sync.dma_start(out=t[:], in_=x_high)
 
         def load_w(j):
             t = raw_pool.tile([P, 2 * 4 * I], BF16, tag="raw", name="wraw%d" % j, align_bytes=256)
@@ -61,12 +69,12 @@ def tile_groupedlinear_kernel(tc, x, W, b, out):
             wraw[j] = t
 
         first = x_pair(0)
-        nc.sync.dma_start(out=first[:, 0, :], in_=xf[0, :, 0, :])
+        nc.sync.dma_start(out=first[:, 0, :], in_=x_low[0, :, 0, :])
         for j in range(4):
             load_w(j)
-        nc.sync.dma_start(out=first[:, 1, :], in_=xf[0, :, 1, :])
-        for n in range(1, NT // 2):
-            load_x_pair(n)
+        nc.sync.dma_start(out=first[:, 1, :], in_=x_low[0, :, 1, :])
+        nc.sync.dma_start(out=x_pair(1)[:], in_=x_low[1])
+        load_x_quad()
 
         ident = const.tile([P, P], F32, name="ident")
         make_identity(nc, ident[:])
@@ -103,7 +111,12 @@ def tile_groupedlinear_kernel(tc, x, W, b, out):
                     for u in range(2):
                         c0 = (2 * j + gg) * 256 + u * P
                         nc.tensor.transpose(tp[:, gg, u, :], xw[:, c0:c0 + P], ident[:])
-                nc.scalar.copy(out=gw[:, 2 * j:2 * j + 2], in_=tp[:].rearrange("p g u r -> p g r u"))
+                dst = gw[:, 2 * j:2 * j + 2]
+                src = tp[:].rearrange("p g u r -> p g r u")
+                if i == 0 and j % 2 == 1:
+                    nc.vector.tensor_copy(out=dst, in_=src)
+                else:
+                    nc.scalar.copy(out=dst, in_=src)
 
         def x_quantise(i):
             q = xq_pool.tile([P, G * P], U32, tag="xq", name="xq%d" % i, align_bytes=64)
@@ -128,7 +141,7 @@ def tile_groupedlinear_kernel(tc, x, W, b, out):
                         nc.tensor.transpose(tp[:, tt, u, :], ww[:, c0:c0 + P], ident[:])
                 dst = gw[:, :, 2 * tpair:2 * tpair + 2, :]
                 src = tp[:].rearrange("p t u r -> p r t u")
-                if tpair < 2:
+                if tpair == 0 or (j == 3 and tpair == 1):
                     nc.vector.tensor_copy(out=dst, in_=src)
                 else:
                     nc.scalar.copy(out=dst, in_=src)
@@ -172,18 +185,18 @@ def tile_groupedlinear_kernel(tc, x, W, b, out):
                     in1=bias[:, hs, gs], op=ADD)
 
         def store(i, h0, h1):
+            dst = o_low[i // 2, :, i % 2] if i < NT // 2 else o_high[:, i - NT // 2]
             nc.sync.dma_start(
-                out=of[i // 2, :, i % 2, h0 * G:h1 * G],
+                out=dst[:, h0 * G:h1 * G],
                 in_=osb[i][:, h0:h1, :].rearrange("p h g -> p (h g)"))
 
         x_transposes(0, 0)
         x_transposes(0, 1)
+        x_quantise(0)
         for j in range(4):
             w_transposes(j)
             bias_block(j)
-            if j == 0:
-                x_quantise(0)
-            else:
+            if j > 0:
                 w_quantise(j - 1)
         x_transposes(1, 0)
         x_transposes(1, 1)
@@ -219,8 +232,7 @@ def tile_groupedlinear_kernel(tc, x, W, b, out):
         bank(i, 0, 1)
         bank(i, 2, 0)
         bank(i, 2, 1)
-        store(i, 0, 256)
-        store(i, 256, 384)
+        store(i, 0, 384)
         bank(i, 3, 0)
         bank(i, 3, 1)
         store(i, 384, 512)

@@ -20,7 +20,7 @@ FLOPS = 2 * TOK * G * I * H
 
 MANUAL = True
 S_BLOCK = 1
-BIG_STORES = 6
+BIG_STORES = 5
 G_SPLIT = 2
 
 
@@ -232,7 +232,8 @@ def tile_groupedlinear_kernel(tc, x, W, b, out):
         bank(i, 0, 1)
         bank(i, 2, 0)
         bank(i, 2, 1)
-        store(i, 0, 384)
+        store(i, 0, 256)
+        store(i, 256, 384)
         bank(i, 3, 0)
         bank(i, 3, 1)
         store(i, 384, 512)

from contextlib import ExitStack

import concourse.mybir as mybir
from concourse.masks import make_identity

F32 = mybir.dt.float32
BF16 = mybir.dt.bfloat16
U32 = mybir.dt.uint32
U8 = mybir.dt.uint8
FP8X4 = mybir.dt.float8_e4m3fn_x4
ADD = mybir.AluOpType.add

P = 128
G = 8
I = 512
H = 512
TOK = 1024
NT = TOK // P
FLOPS = 2 * TOK * G * I * H

MANUAL = True
S_BLOCK = 1
BIG_STORES = 5
G_SPLIT = 2


def tile_groupedlinear_kernel(tc, x, W, b, out):
    nc = tc.nc
    xf = x.flatten_outer_dims()
    of = out.flatten_outer_dims()
    half = TOK // 2
    x_low = xf[0:half, :].rearrange("(n p t) k -> n p t k", p=P, t=2)
    o_low = of[0:half, :].rearrange("(n p t) c -> n p t c", p=P, t=2)
    x_high = xf[half:TOK, :].rearrange("(p t) k -> p t k", t=4)
    o_high = of[half:TOK, :].rearrange("(p t) c -> p t c", t=4)
    with ExitStack() as ctx:
        const = ctx.enter_context(tc.tile_pool(name="const", bufs=1))
        raw_pool = ctx.enter_context(tc.tile_pool(name="raw", bufs=4))
        grp_pool = ctx.enter_context(tc.tile_pool(name="grp", bufs=3))
        xq_pool = ctx.enter_context(tc.tile_pool(name="xq", bufs=2))
        out_pool = ctx.enter_context(tc.tile_pool(name="outp", bufs=4))
        psum_t = ctx.enter_context(tc.psum_pool(name="pt", bufs=4))
        psum_a = ctx.enter_context(tc.psum_pool(name="pa", bufs=4))
        if MANUAL:
            ctx.enter_context(tc.manual_schedule())

        brow = grp_pool.tile([1, G * H], BF16, tag="grp", name="brow", align_bytes=64)
        nc.scalar.dma_start(out=brow[:], in_=b.rearrange("(o g) h -> o (g h)", o=1))

        xraw = {}
        wraw = {}

        def x_pair(n):
            t = raw_pool.tile([P, 2, G * I], BF16, tag="xraw", bufs=2, name="xraw%d" % n, align_bytes=256)
            xraw[2 * n] = t[:, 0, :]
            xraw[2 * n + 1] = t[:, 1, :]
            return t

        def load_x_quad():
            t = raw_pool.tile([P, 4, G * I], BF16, tag="xquad", bufs=1, name="xquad", align_bytes=256)
            for k in range(4):
                xraw[4 + k] = t[:, k, :]
            nc.sync.dma_start(out=t[:], in_=x_high)

        def load_w(j):
            t = raw_pool.tile([P, 2 * 4 * I], BF16, tag="raw", name="wraw%d" % j, align_bytes=256)
            nc.sync.dma_start(
                out=t[:], in_=W[2 * j:2 * j + 2].rearrange("g (q t) i -> (g q) (t i)", t=8))
            wraw[j] = t

        first = x_pair(0)
        nc.sync.dma_start(out=first[:, 0, :], in_=x_low[0, :, 0, :])
        for j in range(4):
            load_w(j)
        nc.sync.dma_start(out=first[:, 1, :], in_=x_low[0, :, 1, :])
        nc.sync.dma_start(out=x_pair(1)[:], in_=x_low[1])
        load_x_quad()

        ident = const.tile([P, P], F32, name="ident")
        make_identity(nc, ident[:])
        ones = const.tile([P, P], BF16, name="ones")
        nc.vector.memset(ones[:], 1.0)
        bz = grp_pool.tile([P, G * H], BF16, tag="grp", name="bz", align_bytes=64)
        nc.vector.memset(bz[:].bitcast(U32), 0)
        nc.vector.tensor_copy(out=bz[0:1, :], in_=brow[:])
        bzv = bz[:].rearrange("p (g h) -> p g h", g=G)
        bias = const.tile([P, H, G], BF16, name="bias")

        def bias_block(hb):
            acc = psum_a.tile([P, G, P], BF16, tag="acc", name="bacc")
            for gh in range(2):
                nc.tensor.matmul(
                    out=acc[:, gh * 4:(gh + 1) * 4, :], lhsT=ones[:],
                    rhs=bzv[:, gh * 4:(gh + 1) * 4, hb * P:(hb + 1) * P],
                    start=True, stop=True)
            nc.scalar.copy(
                out=bias[:, hb * P:(hb + 1) * P, :], in_=acc[:].rearrange("p g h -> p h g"))

        xq = {}
        xs = {}
        xg = {}

        def x_transposes(i, half):
            xw = xraw[i].bitcast(F32)
            if half == 0:
                xg[i] = grp_pool.tile([P, G * I], BF16, tag="grp", name="xg%d" % i, align_bytes=64)
            gw = xg[i][:].bitcast(F32).rearrange("p (g r u) -> p g r u", g=G, u=2)
            for j in range(2 * half, 2 * half + 2):
                tp = psum_t.tile([P, 2, 2, P], F32, tag="tp", name="xtp")
                for gg in range(2):
                    for u in range(2):
                        c0 = (2 * j + gg) * 256 + u * P
                        nc.tensor.transpose(tp[:, gg, u, :], xw[:, c0:c0 + P], ident[:])
                dst = gw[:, 2 * j:2 * j + 2]
                src = tp[:].rearrange("p g u r -> p g r u")
                if i == 0 and j % 2 == 1:
                    nc.vector.tensor_copy(out=dst, in_=src)
                else:
                    nc.scalar.copy(out=dst, in_=src)

        def x_quantise(i):
            q = xq_pool.tile([P, G * P], U32, tag="xq", name="xq%d" % i, align_bytes=64)
            s = xq_pool.tile([P, G * P], U8, tag="xs", name="xs%d" % i, align_bytes=64)
            nc.vector.quantize_mx(out=q[:].bitcast(FP8X4), scales=s[:], in_=xg[i][:])
            xq[i] = q
            xs[i] = s

        wq = {}
        ws = {}
        wg = {}

        def w_transposes(j):
            ww = wraw[j][:].bitcast(F32)
            g_t = grp_pool.tile([P, 2 * H * 4], BF16, tag="grp", name="wg%d" % j, align_bytes=64)
            gw = g_t[:].bitcast(F32).rearrange("p (r t u) -> p r t u", t=8, u=2)
            for tpair in range(4):
                tp = psum_t.tile([P, 2, 2, P], F32, tag="tp", name="wtp")
                for tt in range(2):
                    for u in range(2):
                        c0 = (2 * tpair + tt) * 256 + u * P
                        nc.tensor.transpose(tp[:, tt, u, :], ww[:, c0:c0 + P], ident[:])
                dst = gw[:, :, 2 * tpair:2 * tpair + 2, :]
                src = tp[:].rearrange("p t u r -> p r t u")
                if tpair == 0 or (j == 3 and tpair == 1):
                    nc.vector.tensor_copy(out=dst, in_=src)
                else:
                    nc.scalar.copy(out=dst, in_=src)
            wg[j] = g_t

        def w_quantise(j):
            q = const.tile([P, 2 * H], U32, name="wq%d" % j, align_bytes=64)
            s = const.tile([P, 2 * H], U8, name="ws%d" % j, align_bytes=64)
            nc.vector.quantize_mx(out=q[:].bitcast(FP8X4), scales=s[:], in_=wg[j][:])
            wq[j] = q
            ws[j] = s

        osb = {}

        def bank(i, hb, gh):
            acc = psum_a.tile([P, 4, P], F32, tag="acc", name="acc")
            for g4 in range(4):
                g = gh * 4 + g4
                wc = (g % 2) * H + hb * P
                nc.tensor.matmul_mx(
                    out=acc[:, g4, :],
                    lhsT=xq[i][:, g * P:(g + 1) * P].bitcast(FP8X4),
                    lhsT_scale=xs[i][:, g * P:(g + 1) * P],
                    rhs=wq[g // 2][:, wc:wc + P].bitcast(FP8X4),
                    rhs_scale=ws[g // 2][:, wc:wc + P],
                    start=True, stop=True)
            hs = slice(hb * P, (hb + 1) * P)
            gs = slice(gh * 4, (gh + 1) * 4)
            if hb == S_BLOCK:
                nc.scalar.copy(out=osb[i][:, hs, gs], in_=acc[:].rearrange("p g h -> p h g"))
                if gh == 1:
                    step = P // G_SPLIT
                    for k in range(G_SPLIT):
                        ks = slice(hb * P + k * step, hb * P + (k + 1) * step)
                        o2 = osb[i][:, ks, :].rearrange("p h g -> p (h g)")
                        nc.gpsimd.tensor_tensor(
                            out=o2, in0=o2, in1=bias[:, ks, :].rearrange("p h g -> p (h g)"), op=ADD)
            else:
                nc.vector.tensor_tensor(
                    out=osb[i][:, hs, gs], in0=acc[:].rearrange("p g h -> p h g"),
                    in1=bias[:, hs, gs], op=ADD)

        def store(i, h0, h1):
            dst = o_low[i // 2, :, i % 2] if i < NT // 2 else o_high[:, i - NT // 2]
            nc.sync.dma_start(
                out=dst[:, h0 * G:h1 * G],
                in_=osb[i][:, h0:h1, :].rearrange("p h g -> p (h g)"))

        x_transposes(0, 0)
        x_transposes(0, 1)
        x_quantise(0)
        for j in range(4):
            w_transposes(j)
            bias_block(j)
            if j > 0:
                w_quantise(j - 1)
        x_transposes(1, 0)
        x_transposes(1, 1)
        w_quantise(3)

        for i in range(NT - 1):
            osb[i] = out_pool.tile([P, H, G], F32, tag="osb", name="osb%d" % i, align_bytes=256)
            bank(i, 0, 0)
            bank(i, 0, 1)
            bank(i, 1, 0)
            bank(i, 1, 1)
            x_quantise(i + 1)
            if i + 2 < NT:
                x_transposes(i + 2, 0)
            bank(i, 2, 0)
            bank(i, 2, 1)
            if i >= BIG_STORES:
                store(i, 0, 256)
            bank(i, 3, 0)
            bank(i, 3, 1)
            if i + 2 < NT:
                x_transposes(i + 2, 1)
            if i >= BIG_STORES:
                store(i, 256, 512)
            else:
                store(i, 0, 512)

        i = NT - 1
        osb[i] = out_pool.tile([P, H, G], F32, tag="osb", name="osb%d" % i, align_bytes=256)
        bank(i, 1, 0)
        bank(i, 0, 0)
        bank(i, 1, 1)
        bank(i, 0, 1)
        bank(i, 2, 0)
        bank(i, 2, 1)
        store(i, 0, 256)
        store(i, 256, 384)
        bank(i, 3, 0)
        bank(i, 3, 1)
        store(i, 384, 512)
